import numpy as np
import ml_dtypes

BF16 = ml_dtypes.bfloat16


def bf(x):
    return np.asarray(x, np.float32).astype(BF16)


def f32(x):
    return np.asarray(x, np.float32)


def f64(x):
    return np.asarray(x).astype(np.float64)


def striped(idx):
    return np.tile(idx.reshape(-1, 16).T, (8, 1))


D, S, N, HQ, HK, M = 128, 4096, 2048, 2, 1, 512
EPS = 1e-5


def head_layernorm(y, gain):
    mu = y.mean(axis=0, keepdims=True)
    var = ((y - mu) ** 2).mean(axis=0, keepdims=True)
    return gain * (y - mu) / np.sqrt(var + EPS)


def setup_inputs():
    return {"table": bf(np.random.standard_normal((D, S))), "w": bf(np.random.standard_normal((D, M)) / np.sqrt(D)), "q_gain": f32(1.0 + 0.1 * np.random.standard_normal((D, 1))), "k_gain": f32(1.0 + 0.1 * np.random.standard_normal((D, 1))), "offs": striped(np.random.permutation(S)[:N])}


def reference(table, w, q_gain, k_gain, offs):
    idx = offs[:16].T.reshape(-1)
    y = f64(w).T @ f64(table)[:, idx]
    res = y.copy()
    for h in range(HQ + HK):
        gain = f64(q_gain) if h < HQ else f64(k_gain)
        res[h * D:(h + 1) * D] = head_layernorm(y[h * D:(h + 1) * D], gain)
    return res

@@ -1,0 +1,103 @@
+import concourse.mybir as mybir
+from concourse.masks import make_identity
+
+BF16, F32, U16 = mybir.dt.bfloat16, mybir.dt.float32, mybir.dt.uint16
+ALU = mybir.AluOpType
+ACT = mybir.ActivationFunctionType
+
+P = 128
+TABLE_COLUMNS = 4096
+PICKED = 2048
+PIECE = 512
+BLOCKS = PIECE // P
+OFFSET_COLUMNS = PIECE // 16
+HEADS = 4
+VALUE_HEAD = 3
+EPS = 1e-5
+
+FLOPS = 2 * P * HEADS * P * PICKED
+
+
+def tile_cohereattention_kernel(tc, table, w, q_gain, k_gain, offs, out):
+    nc = tc.nc
+    with (
+        tc.tile_pool(name="held", bufs=1) as held,
+        tc.tile_pool(name="work", bufs=3) as work,
+        tc.tile_pool(name="small", bufs=4) as small,
+        tc.psum_pool(name="psum", bufs=2) as psum,
+    ):
+        offsets = held.tile([P, PICKED // 16], U16, name="offsets")
+        nc.sync.dma_start(offsets[:], offs)
+        weights = held.tile([P, HEADS * P], BF16, name="weights")
+        nc.scalar.dma_start(weights[:], w)
+        window = held.tile([P, TABLE_COLUMNS], BF16, name="window")
+        half = TABLE_COLUMNS // 2
+        nc.sync.dma_start(window[:, :half], table[:, :half])
+        nc.scalar.dma_start(window[:, half:], table[:, half:])
+        query_gain = held.tile([P, 1], F32, name="query_gain")
+        nc.sync.dma_start(query_gain[:], q_gain)
+        key_gain = held.tile([P, 1], F32, name="key_gain")
+        nc.sync.dma_start(key_gain[:], k_gain)
+        gain_of_head = [query_gain, query_gain, key_gain]
+
+        identity = held.tile([P, P], F32, name="identity")
+        make_identity(nc, identity[:])
+        minus_half = held.tile([P, BLOCKS], F32, name="minus_half")
+        nc.gpsimd.memset(minus_half[:], -0.5)
+
+        for piece in range(PICKED // PIECE):
+            piece_offsets = offsets[:, piece * OFFSET_COLUMNS : (piece + 1) * OFFSET_COLUMNS]
+            for head in range(HEADS):
+                product = psum.tile([P, PIECE], F32, name="product", bufs=3)
+                nc.tensor.matmul(
+                    product[:],
+                    weights[:, head * P : (head + 1) * P],
+                    window[:].indirect(piece_offsets),
+                    start=True,
+                    stop=True,
+                )
+                result = work.tile([P, PIECE], F32, name="result")
+
+                if head == VALUE_HEAD:
+                    nc.scalar.activation(result[:], product[:], ACT.Copy)
+                else:
+                    product_sb = work.tile([P, PIECE], F32, name="product_sb")
+                    nc.scalar.activation(product_sb[:], product[:], ACT.Copy)
+                    by_token = psum.tile([P, BLOCKS, P], F32, name="by_token", bufs=3)
+                    for b in range(BLOCKS):
+                        nc.tensor.transpose(
+                            by_token[:, b, :], product_sb[:, b * P : (b + 1) * P], identity[:]
+                        )
+
+                    stats = small.tile([P, BLOCKS, 6], F32, name="stats")
+                    mean_var = small.tile([P, BLOCKS, 2], F32, name="mean_var")
+                    for b in range(BLOCKS):
+                        nc.vector.bn_stats(stats[:, b, :], by_token[:, b, :])
+                        nc.vector.bn_aggr(mean_var[:, b, :], stats[:, b, :])
+                    var_eps = small.tile([P, BLOCKS], F32, name="var_eps")
+                    nc.gpsimd.tensor_scalar_add(var_eps[:], mean_var[:, :, 1], EPS)
+                    inv_std = small.tile([P, BLOCKS], F32, name="inv_std")
+                    nc.gpsimd.tensor_tensor(inv_std[:], var_eps[:], minus_half[:], ALU.pow)
+
+                    normed = work.tile([P, BLOCKS, P], F32, name="normed")
+                    for b in range(BLOCKS):
+                        nc.vector.tensor_scalar(
+                            normed[:, b, :],
+                            by_token[:, b, :],
+                            mean_var[:, b, 0:1],
+                            inv_std[:, b : b + 1],
+                            ALU.subtract,
+                            ALU.mult,
+                        )
+                    by_feature = psum.tile([P, PIECE], F32, name="by_feature", bufs=2)
+                    for b in range(BLOCKS):
+                        nc.tensor.transpose(
+                            by_feature[:, b * P : (b + 1) * P], normed[:, b, :], identity[:]
+                        )
+                    nc.scalar.activation(
+                        result[:], by_feature[:], ACT.Identity, scale=gain_of_head[head][:, 0:1]
+                    )
+
+                nc.sync.dma_start(
+                    out[head * P : (head + 1) * P, piece * PIECE : (piece + 1) * PIECE], result[:]
+                )

@@ -22,7 +22,7 @@ def tile_cohereattention_kernel(tc, table, w, q_gain, k_gain, offs, out):
     nc = tc.nc
     with (
         tc.tile_pool(name="held", bufs=1) as held,
-        tc.tile_pool(name="work", bufs=3) as work,
+        tc.tile_pool(name="work", bufs=4) as work,
         tc.tile_pool(name="small", bufs=4) as small,
         tc.psum_pool(name="psum", bufs=2) as psum,
     ):
@@ -56,10 +56,9 @@ def tile_cohereattention_kernel(tc, table, w, q_gain, k_gain, offs, out):
                     start=True,
                     stop=True,
                 )
-                result = work.tile([P, PIECE], F32, name="result")
-
                 if head == VALUE_HEAD:
-                    nc.scalar.activation(result[:], product[:], ACT.Copy)
+                    result = work.tile([P, PIECE], F32, name="result")
+                    nc.vector.tensor_copy(result[:], product[:])
                 else:
                     product_sb = work.tile([P, PIECE], F32, name="product_sb")
                     nc.scalar.activation(product_sb[:], product[:], ACT.Copy)
@@ -75,7 +74,7 @@ def tile_cohereattention_kernel(tc, table, w, q_gain, k_gain, offs, out):
                         nc.vector.bn_stats(stats[:, b, :], by_token[:, b, :])
                         nc.vector.bn_aggr(mean_var[:, b, :], stats[:, b, :])
                     var_eps = small.tile([P, BLOCKS], F32, name="var_eps")
-                    nc.gpsimd.tensor_scalar_add(var_eps[:], mean_var[:, :, 1], EPS)
+                    nc.vector.tensor_scalar_add(var_eps[:], mean_var[:, :, 1], EPS)
                     inv_std = small.tile([P, BLOCKS], F32, name="inv_std")
                     nc.gpsimd.tensor_tensor(inv_std[:], var_eps[:], minus_half[:], ALU.pow)
 
@@ -94,6 +93,7 @@ def tile_cohereattention_kernel(tc, table, w, q_gain, k_gain, offs, out):
                         nc.tensor.transpose(
                             by_feature[:, b * P : (b + 1) * P], normed[:, b, :], identity[:]
                         )
+                    result = work.tile([P, PIECE], F32, name="result")
                     nc.scalar.activation(
                         result[:], by_feature[:], ACT.Identity, scale=gain_of_head[head][:, 0:1]
                     )

@@ -42,8 +42,10 @@ def tile_cohereattention_kernel(tc, table, w, q_gain, k_gain, offs, out):
 
         identity = held.tile([P, P], F32, name="identity")
         make_identity(nc, identity[:])
-        minus_half = held.tile([P, BLOCKS], F32, name="minus_half")
-        nc.gpsimd.memset(minus_half[:], -0.5)
+        eps = held.tile([P, 1], F32, name="eps")
+        nc.vector.memset(eps[:], EPS)
+        scratch = held.tile([P, 1], F32, name="scratch")
+        nc.scalar.activation(scratch[:], eps[:], ACT.Sqrt)
 
         for piece in range(PICKED // PIECE):
             piece_offsets = offsets[:, piece * OFFSET_COLUMNS : (piece + 1) * OFFSET_COLUMNS]
@@ -73,10 +75,10 @@ def tile_cohereattention_kernel(tc, table, w, q_gain, k_gain, offs, out):
                     for b in range(BLOCKS):
                         nc.vector.bn_stats(stats[:, b, :], by_token[:, b, :])
                         nc.vector.bn_aggr(mean_var[:, b, :], stats[:, b, :])
-                    var_eps = small.tile([P, BLOCKS], F32, name="var_eps")
-                    nc.vector.tensor_scalar_add(var_eps[:], mean_var[:, :, 1], EPS)
+                    std = small.tile([P, BLOCKS], F32, name="std")
+                    nc.scalar.activation(std[:], mean_var[:, :, 1], ACT.Sqrt, bias=eps[:, 0:1])
                     inv_std = small.tile([P, BLOCKS], F32, name="inv_std")
-                    nc.gpsimd.tensor_tensor(inv_std[:], var_eps[:], minus_half[:], ALU.pow)
+                    nc.vector.reciprocal(inv_std[:], std[:])
 
                     normed = work.tile([P, BLOCKS, P], F32, name="normed")
                     for b in range(BLOCKS):

@@ -9,11 +9,13 @@ P = 128
 TABLE_COLUMNS = 4096
 PICKED = 2048
 PIECE = 512
+PIECES = PICKED // PIECE
 BLOCKS = PIECE // P
 OFFSET_COLUMNS = PIECE // 16
 HEADS = 4
 VALUE_HEAD = 3
 EPS = 1e-5
+PSUM_BANKS = 8
 
 FLOPS = 2 * P * HEADS * P * PICKED
 
@@ -24,7 +26,7 @@ def tile_cohereattention_kernel(tc, table, w, q_gain, k_gain, offs, out):
         tc.tile_pool(name="held", bufs=1) as held,
         tc.tile_pool(name="work", bufs=4) as work,
         tc.tile_pool(name="small", bufs=4) as small,
-        tc.psum_pool(name="psum", bufs=2) as psum,
+        tc.psum_pool(name="psum", bufs=PSUM_BANKS) as psum,
     ):
         offsets = held.tile([P, PICKED // 16], U16, name="offsets")
         nc.sync.dma_start(offsets[:], offs)
@@ -47,59 +49,74 @@ def tile_cohereattention_kernel(tc, table, w, q_gain, k_gain, offs, out):
         scratch = held.tile([P, 1], F32, name="scratch")
         nc.scalar.activation(scratch[:], eps[:], ACT.Sqrt)
 
-        for piece in range(PICKED // PIECE):
-            piece_offsets = offsets[:, piece * OFFSET_COLUMNS : (piece + 1) * OFFSET_COLUMNS]
-            for head in range(HEADS):
-                product = psum.tile([P, PIECE], F32, name="product", bufs=3)
-                nc.tensor.matmul(
-                    product[:],
-                    weights[:, head * P : (head + 1) * P],
-                    window[:].indirect(piece_offsets),
-                    start=True,
-                    stop=True,
+        def project(piece, head):
+            product = psum.tile([P, PIECE], F32, name="product", tag="bank")
+            nc.tensor.matmul(
+                product[:],
+                weights[:, head * P : (head + 1) * P],
+                window[:].indirect(offsets[:, piece * OFFSET_COLUMNS : (piece + 1) * OFFSET_COLUMNS]),
+                start=True,
+                stop=True,
+            )
+            return product
+
+        def store(piece, head, result):
+            nc.sync.dma_start(
+                out[head * P : (head + 1) * P, piece * PIECE : (piece + 1) * PIECE], result[:]
+            )
+
+        to_normalise = [(piece, head) for piece in range(PIECES) for head in range(VALUE_HEAD)]
+
+        parked = []
+        for n, (piece, head) in enumerate(to_normalise):
+            product = project(piece, head)
+            product_sb = held.tile([P, PIECE], F32, name=f"product_sb{n}")
+            if n % 2 == 0:
+                nc.scalar.activation(product_sb[:], product[:], ACT.Copy)
+            else:
+                nc.vector.tensor_copy(product_sb[:], product[:])
+            parked.append(product_sb)
+
+        for (piece, head), product_sb in zip(to_normalise, parked):
+            by_token = psum.tile([P, BLOCKS, P], F32, name="by_token", tag="bank")
+            for b in range(BLOCKS):
+                nc.tensor.transpose(
+                    by_token[:, b, :], product_sb[:, b * P : (b + 1) * P], identity[:]
                 )
-                if head == VALUE_HEAD:
-                    result = work.tile([P, PIECE], F32, name="result")
-                    nc.vector.tensor_copy(result[:], product[:])
-                else:
-                    product_sb = work.tile([P, PIECE], F32, name="product_sb")
-                    nc.scalar.activation(product_sb[:], product[:], ACT.Copy)
-                    by_token = psum.tile([P, BLOCKS, P], F32, name="by_token", bufs=3)
-                    for b in range(BLOCKS):
-                        nc.tensor.transpose(
-                            by_token[:, b, :], product_sb[:, b * P : (b + 1) * P], identity[:]
-                        )
 
-                    stats = small.tile([P, BLOCKS, 6], F32, name="stats")
-                    mean_var = small.tile([P, BLOCKS, 2], F32, name="mean_var")
-                    for b in range(BLOCKS):
-                        nc.vector.bn_stats(stats[:, b, :], by_token[:, b, :])
-                        nc.vector.bn_aggr(mean_var[:, b, :], stats[:, b, :])
-                    std = small.tile([P, BLOCKS], F32, name="std")
-                    nc.scalar.activation(std[:], mean_var[:, :, 1], ACT.Sqrt, bias=eps[:, 0:1])
-                    inv_std = small.tile([P, BLOCKS], F32, name="inv_std")
-                    nc.vector.reciprocal(inv_std[:], std[:])
+            stats = small.tile([P, BLOCKS, 6], F32, name="stats")
+            mean_var = small.tile([P, BLOCKS, 2], F32, name="mean_var")
+            for b in range(BLOCKS):
+                nc.vector.bn_stats(stats[:, b, :], by_token[:, b, :])
+                nc.vector.bn_aggr(mean_var[:, b, :], stats[:, b, :])
+            std = small.tile([P, BLOCKS], F32, name="std")
+            nc.scalar.activation(std[:], mean_var[:, :, 1], ACT.Sqrt, bias=eps[:, 0:1])
+            inv_std = small.tile([P, BLOCKS], F32, name="inv_std")
+            nc.vector.reciprocal(inv_std[:], std[:])
 
-                    normed = work.tile([P, BLOCKS, P], F32, name="normed")
-                    for b in range(BLOCKS):
-                        nc.vector.tensor_scalar(
-                            normed[:, b, :],
-                            by_token[:, b, :],
-                            mean_var[:, b, 0:1],
-                            inv_std[:, b : b + 1],
-                            ALU.subtract,
-                            ALU.mult,
-                        )
-                    by_feature = psum.tile([P, PIECE], F32, name="by_feature", bufs=2)
-                    for b in range(BLOCKS):
-                        nc.tensor.transpose(
-                            by_feature[:, b * P : (b + 1) * P], normed[:, b, :], identity[:]
-                        )
-                    result = work.tile([P, PIECE], F32, name="result")
-                    nc.scalar.activation(
-                        result[:], by_feature[:], ACT.Identity, scale=gain_of_head[head][:, 0:1]
-                    )
-
-                nc.sync.dma_start(
-                    out[head * P : (head + 1) * P, piece * PIECE : (piece + 1) * PIECE], result[:]
+            normed = work.tile([P, BLOCKS, P], F32, name="normed")
+            for b in range(BLOCKS):
+                nc.vector.tensor_scalar(
+                    normed[:, b, :],
+                    by_token[:, b, :],
+                    mean_var[:, b, 0:1],
+                    inv_std[:, b : b + 1],
+                    ALU.subtract,
+                    ALU.mult,
                 )
+            by_feature = psum.tile([P, PIECE], F32, name="by_feature", tag="bank")
+            for b in range(BLOCKS):
+                nc.tensor.transpose(
+                    by_feature[:, b * P : (b + 1) * P], normed[:, b, :], identity[:]
+                )
+            result = work.tile([P, PIECE], F32, name="result")
+            nc.scalar.activation(
+                result[:], by_feature[:], ACT.Identity, scale=gain_of_head[head][:, 0:1]
+            )
+            store(piece, head, result)
+
+        for piece in range(PIECES):
+            product = project(piece, VALUE_HEAD)
+            value = work.tile([P, PIECE], F32, name="value")
+            nc.scalar.activation(value[:], product[:], ACT.Copy)
+            store(piece, VALUE_HEAD, value)

@@ -16,6 +16,8 @@ HEADS = 4
 VALUE_HEAD = 3
 EPS = 1e-5
 PSUM_BANKS = 8
+WARM_UP_MATMULS = 10
+BACK_BANKS = 2
 
 FLOPS = 2 * P * HEADS * P * PICKED
 
@@ -26,7 +28,7 @@ def tile_cohereattention_kernel(tc, table, w, q_gain, k_gain, offs, out):
         tc.tile_pool(name="held", bufs=1) as held,
         tc.tile_pool(name="work", bufs=4) as work,
         tc.tile_pool(name="small", bufs=4) as small,
-        tc.psum_pool(name="psum", bufs=PSUM_BANKS) as psum,
+        tc.psum_pool(name="psum", bufs=PSUM_BANKS - BACK_BANKS) as psum,
     ):
         offsets = held.tile([P, PICKED // 16], U16, name="offsets")
         nc.sync.dma_start(offsets[:], offs)
@@ -48,6 +50,12 @@ def tile_cohereattention_kernel(tc, table, w, q_gain, k_gain, offs, out):
         nc.vector.memset(eps[:], EPS)
         scratch = held.tile([P, 1], F32, name="scratch")
         nc.scalar.activation(scratch[:], eps[:], ACT.Sqrt)
+
+        zeros = held.tile([P, PIECE], BF16, name="zeros")
+        nc.vector.memset(zeros[:], 0.0)
+        unread = psum.tile([P, PIECE], F32, name="unread", tag="bank")
+        for step in range(WARM_UP_MATMULS):
+            nc.tensor.matmul(unread[:], zeros[:, :P], zeros[:], start=True, stop=True)
 
         def project(piece, head):
             product = psum.tile([P, PIECE], F32, name="product", tag="bank")
@@ -104,7 +112,7 @@ def tile_cohereattention_kernel(tc, table, w, q_gain, k_gain, offs, out):
                     ALU.subtract,
                     ALU.mult,
                 )
-            by_feature = psum.tile([P, PIECE], F32, name="by_feature", tag="bank")
+            by_feature = psum.tile([P, PIECE], F32, name="by_feature", bufs=BACK_BANKS)
             for b in range(BLOCKS):
                 nc.tensor.transpose(
                     by_feature[:, b * P : (b + 1) * P], normed[:, b, :], identity[:]

@@ -75,18 +75,25 @@ def tile_cohereattention_kernel(tc, table, w, q_gain, k_gain, offs, out):
 
         to_normalise = [(piece, head) for piece in range(PIECES) for head in range(VALUE_HEAD)]
 
+        every_product = [(piece, head) for piece in range(PIECES) for head in range(HEADS)]
         parked = []
-        for n, (piece, head) in enumerate(to_normalise):
+        for n, (piece, head) in enumerate(every_product):
             product = project(piece, head)
             product_sb = held.tile([P, PIECE], F32, name=f"product_sb{n}")
             if n % 2 == 0:
                 nc.scalar.activation(product_sb[:], product[:], ACT.Copy)
             else:
                 nc.vector.tensor_copy(product_sb[:], product[:])
-            parked.append(product_sb)
+            if head == VALUE_HEAD:
+                store(piece, head, product_sb)
+            else:
+                parked.append(product_sb)
 
         for (piece, head), product_sb in zip(to_normalise, parked):
             by_token = psum.tile([P, BLOCKS, P], F32, name="by_token", tag="bank")
+            nc.tensor.matmul(
+                by_token[:].rearrange("p b x -> p (b x)"), zeros[:, :P], zeros[:], start=True, stop=True
+            )
             for b in range(BLOCKS):
                 nc.tensor.transpose(
                     by_token[:, b, :], product_sb[:, b * P : (b + 1) * P], identity[:]
@@ -113,6 +120,7 @@ def tile_cohereattention_kernel(tc, table, w, q_gain, k_gain, offs, out):
                     ALU.mult,
                 )
             by_feature = psum.tile([P, PIECE], F32, name="by_feature", bufs=BACK_BANKS)
+            nc.tensor.matmul(by_feature[:], zeros[:, :P], zeros[:], start=True, stop=True)
             for b in range(BLOCKS):
                 nc.tensor.transpose(
                     by_feature[:, b * P : (b + 1) * P], normed[:, b, :], identity[:]
@@ -122,9 +130,3 @@ def tile_cohereattention_kernel(tc, table, w, q_gain, k_gain, offs, out):
                 result[:], by_feature[:], ACT.Identity, scale=gain_of_head[head][:, 0:1]
             )
             store(piece, head, result)
-
-        for piece in range(PIECES):
-            product = project(piece, VALUE_HEAD)
-            value = work.tile([P, PIECE], F32, name="value")
-            nc.scalar.activation(value[:], product[:], ACT.Copy)
-            store(piece, VALUE_HEAD, value)

@@ -9,15 +9,15 @@ P = 128
 TABLE_COLUMNS = 4096
 PICKED = 2048
 PIECE = 512
-PIECES = PICKED // PIECE
-BLOCKS = PIECE // P
 OFFSET_COLUMNS = PIECE // 16
+SIDE = 32
+FOUR = P // SIDE
 HEADS = 4
 VALUE_HEAD = 3
 EPS = 1e-5
+NORMALISED = VALUE_HEAD * (PICKED // PIECE)
 PSUM_BANKS = 8
 WARM_UP_MATMULS = 10
-BACK_BANKS = 2
 
 FLOPS = 2 * P * HEADS * P * PICKED
 
@@ -26,9 +26,9 @@ def tile_cohereattention_kernel(tc, table, w, q_gain, k_gain, offs, out):
     nc = tc.nc
     with (
         tc.tile_pool(name="held", bufs=1) as held,
-        tc.tile_pool(name="work", bufs=4) as work,
-        tc.tile_pool(name="small", bufs=4) as small,
-        tc.psum_pool(name="psum", bufs=PSUM_BANKS - BACK_BANKS) as psum,
+        tc.tile_pool(name="work", bufs=NORMALISED) as work,
+        tc.tile_pool(name="small", bufs=NORMALISED) as small,
+        tc.psum_pool(name="psum", bufs=PSUM_BANKS) as psum,
     ):
         offsets = held.tile([P, PICKED // 16], U16, name="offsets")
         nc.sync.dma_start(offsets[:], offs)
@@ -38,11 +38,6 @@ def tile_cohereattention_kernel(tc, table, w, q_gain, k_gain, offs, out):
         half = TABLE_COLUMNS // 2
         nc.sync.dma_start(window[:, :half], table[:, :half])
         nc.scalar.dma_start(window[:, half:], table[:, half:])
-        query_gain = held.tile([P, 1], F32, name="query_gain")
-        nc.sync.dma_start(query_gain[:], q_gain)
-        key_gain = held.tile([P, 1], F32, name="key_gain")
-        nc.sync.dma_start(key_gain[:], k_gain)
-        gain_of_head = [query_gain, query_gain, key_gain]
 
         identity = held.tile([P, P], F32, name="identity")
         make_identity(nc, identity[:])
@@ -50,6 +45,15 @@ def tile_cohereattention_kernel(tc, table, w, q_gain, k_gain, offs, out):
         nc.vector.memset(eps[:], EPS)
         scratch = held.tile([P, 1], F32, name="scratch")
         nc.scalar.activation(scratch[:], eps[:], ACT.Sqrt)
+
+        gain_of_head = []
+        for name, gain in (("query", q_gain), ("key", k_gain)):
+            gain_rows = held.tile([P, P], F32, name=name + "_gain_rows", align_bytes=64)
+            nc.sync.dma_start(gain_rows[:], gain.rearrange("r one -> (r one)").partition_broadcast(P))
+            gain_by_lane = held.tile([P, P], F32, name=name + "_gain_by_lane", align_bytes=64)
+            nc.vector.transpose(gain_by_lane[:], gain_rows[:])
+            gain_of_head.append(gain_by_lane)
+        gain_of_head.insert(0, gain_of_head[0])
 
         zeros = held.tile([P, PIECE], BF16, name="zeros")
         nc.vector.memset(zeros[:], 0.0)
@@ -68,65 +72,72 @@ def tile_cohereattention_kernel(tc, table, w, q_gain, k_gain, offs, out):
             )
             return product
 
-        def store(piece, head, result):
-            nc.sync.dma_start(
-                out[head * P : (head + 1) * P, piece * PIECE : (piece + 1) * PIECE], result[:]
-            )
+        to_normalise = [(piece, head) for piece in range(PICKED // PIECE) for head in range(VALUE_HEAD)]
 
-        to_normalise = [(piece, head) for piece in range(PIECES) for head in range(VALUE_HEAD)]
-
-        every_product = [(piece, head) for piece in range(PIECES) for head in range(HEADS)]
         parked = []
-        for n, (piece, head) in enumerate(every_product):
+        for piece, head in to_normalise:
             product = project(piece, head)
-            product_sb = held.tile([P, PIECE], F32, name=f"product_sb{n}")
-            if n % 2 == 0:
-                nc.scalar.activation(product_sb[:], product[:], ACT.Copy)
-            else:
-                nc.vector.tensor_copy(product_sb[:], product[:])
-            if head == VALUE_HEAD:
-                store(piece, head, product_sb)
-            else:
-                parked.append(product_sb)
+            product_sb = work.tile([P, PIECE], F32, name="product_sb")
+            nc.scalar.activation(
+                product_sb[:].rearrange("r (g q b) -> r g q b", g=FOUR, q=FOUR),
+                product[:].rearrange("r (q g b) -> r g q b", q=FOUR, g=FOUR),
+                ACT.Copy,
+            )
+            parked.append(product_sb)
 
         for (piece, head), product_sb in zip(to_normalise, parked):
-            by_token = psum.tile([P, BLOCKS, P], F32, name="by_token", tag="bank")
-            nc.tensor.matmul(
-                by_token[:].rearrange("p b x -> p (b x)"), zeros[:, :P], zeros[:], start=True, stop=True
-            )
-            for b in range(BLOCKS):
+            by_token = psum.tile([P, FOUR, P], F32, name="by_token", tag="bank")
+            for g in range(FOUR):
                 nc.tensor.transpose(
-                    by_token[:, b, :], product_sb[:, b * P : (b + 1) * P], identity[:]
+                    by_token[:, g, :], product_sb[:, g * P : (g + 1) * P], identity[:]
                 )
 
-            stats = small.tile([P, BLOCKS, 6], F32, name="stats")
-            mean_var = small.tile([P, BLOCKS, 2], F32, name="mean_var")
-            for b in range(BLOCKS):
-                nc.vector.bn_stats(stats[:, b, :], by_token[:, b, :])
-                nc.vector.bn_aggr(mean_var[:, b, :], stats[:, b, :])
-            std = small.tile([P, BLOCKS], F32, name="std")
+            stats = small.tile([P, FOUR, 6], F32, name="stats")
+            mean_var = small.tile([P, FOUR, 2], F32, name="mean_var")
+            for g in range(FOUR):
+                nc.vector.bn_stats(stats[:, g, :], by_token[:, g, :])
+                nc.vector.bn_aggr(mean_var[:, g, :], stats[:, g, :])
+            std = small.tile([P, FOUR], F32, name="std")
             nc.scalar.activation(std[:], mean_var[:, :, 1], ACT.Sqrt, bias=eps[:, 0:1])
-            inv_std = small.tile([P, BLOCKS], F32, name="inv_std")
+            inv_std = small.tile([P, FOUR], F32, name="inv_std")
             nc.vector.reciprocal(inv_std[:], std[:])
-
-            normed = work.tile([P, BLOCKS, P], F32, name="normed")
-            for b in range(BLOCKS):
-                nc.vector.tensor_scalar(
-                    normed[:, b, :],
-                    by_token[:, b, :],
-                    mean_var[:, b, 0:1],
-                    inv_std[:, b : b + 1],
-                    ALU.subtract,
-                    ALU.mult,
-                )
-            by_feature = psum.tile([P, PIECE], F32, name="by_feature", bufs=BACK_BANKS)
-            nc.tensor.matmul(by_feature[:], zeros[:, :P], zeros[:], start=True, stop=True)
-            for b in range(BLOCKS):
-                nc.tensor.transpose(
-                    by_feature[:, b * P : (b + 1) * P], normed[:, b, :], identity[:]
-                )
-            result = work.tile([P, PIECE], F32, name="result")
-            nc.scalar.activation(
-                result[:], by_feature[:], ACT.Identity, scale=gain_of_head[head][:, 0:1]
+            shift = small.tile([P, FOUR], F32, name="shift")
+            nc.vector.scalar_tensor_tensor(
+                shift[:], mean_var[:, :, 0], -1.0, inv_std[:], ALU.mult, ALU.mult
             )
-            store(piece, head, result)
+
+            normed = work.tile([P, FOUR, FOUR, SIDE], F32, name="normed", align_bytes=64)
+            for g in range(FOUR):
+                nc.scalar.activation(
+                    normed[:, :, g, :],
+                    by_token[:, g, :].rearrange("p (c a) -> p c a", c=FOUR),
+                    ACT.Identity,
+                    bias=shift[:, g : g + 1],
+                    scale=inv_std[:, g : g + 1],
+                )
+            flipped = work.tile([P, FOUR, P], F32, name="flipped", align_bytes=64)
+            nc.vector.transpose(
+                flipped[:].rearrange("p c x -> p (c x)"),
+                normed[:].rearrange("p c g a -> p (c g a)"),
+            )
+            result = work.tile([P, FOUR, P], F32, name="result")
+            for c in range(FOUR):
+                nc.vector.tensor_scalar_mul(
+                    result[:, c, :],
+                    flipped[:, c, :],
+                    gain_of_head[head][:, c * SIDE : c * SIDE + 1],
+                )
+            rows = out[head * P : (head + 1) * P, piece * PIECE : (piece + 1) * PIECE]
+            for q in range(FOUR):
+                nc.sync.dma_start(
+                    rows[:, q * P : (q + 1) * P].rearrange("(c a) x -> a c x", c=FOUR),
+                    result[q * SIDE : (q + 1) * SIDE, :, :],
+                )
+
+        for piece in range(PICKED // PIECE):
+            product = project(piece, VALUE_HEAD)
+            value = work.tile([P, PIECE], F32, name="value")
+            nc.scalar.activation(value[:], product[:], ACT.Copy)
+            nc.sync.dma_start(
+                out[VALUE_HEAD * P : HEADS * P, piece * PIECE : (piece + 1) * PIECE], value[:]
+            )

@@ -9,15 +9,16 @@ P = 128
 TABLE_COLUMNS = 4096
 PICKED = 2048
 PIECE = 512
+PIECES = PICKED // PIECE
+BLOCKS = PIECE // P
 OFFSET_COLUMNS = PIECE // 16
-SIDE = 32
-FOUR = P // SIDE
 HEADS = 4
 VALUE_HEAD = 3
 EPS = 1e-5
-NORMALISED = VALUE_HEAD * (PICKED // PIECE)
 PSUM_BANKS = 8
+IN_FLIGHT = 4
 WARM_UP_MATMULS = 10
+BACK_BANKS = 2
 
 FLOPS = 2 * P * HEADS * P * PICKED
 
@@ -26,9 +27,9 @@ def tile_cohereattention_kernel(tc, table, w, q_gain, k_gain, offs, out):
     nc = tc.nc
     with (
         tc.tile_pool(name="held", bufs=1) as held,
-        tc.tile_pool(name="work", bufs=NORMALISED) as work,
-        tc.tile_pool(name="small", bufs=NORMALISED) as small,
-        tc.psum_pool(name="psum", bufs=PSUM_BANKS) as psum,
+        tc.tile_pool(name="work", bufs=IN_FLIGHT) as work,
+        tc.tile_pool(name="small", bufs=IN_FLIGHT) as small,
+        tc.psum_pool(name="psum", bufs=PSUM_BANKS - BACK_BANKS) as psum,
     ):
         offsets = held.tile([P, PICKED // 16], U16, name="offsets")
         nc.sync.dma_start(offsets[:], offs)
@@ -38,6 +39,11 @@ def tile_cohereattention_kernel(tc, table, w, q_gain, k_gain, offs, out):
         half = TABLE_COLUMNS // 2
         nc.sync.dma_start(window[:, :half], table[:, :half])
         nc.scalar.dma_start(window[:, half:], table[:, half:])
+        query_gain = held.tile([P, 1], F32, name="query_gain")
+        nc.sync.dma_start(query_gain[:], q_gain)
+        key_gain = held.tile([P, 1], F32, name="key_gain")
+        nc.sync.dma_start(key_gain[:], k_gain)
+        gain_of_head = [query_gain, query_gain, key_gain]
 
         identity = held.tile([P, P], F32, name="identity")
         make_identity(nc, identity[:])
@@ -45,15 +51,6 @@ def tile_cohereattention_kernel(tc, table, w, q_gain, k_gain, offs, out):
         nc.vector.memset(eps[:], EPS)
         scratch = held.tile([P, 1], F32, name="scratch")
         nc.scalar.activation(scratch[:], eps[:], ACT.Sqrt)
-
-        gain_of_head = []
-        for name, gain in (("query", q_gain), ("key", k_gain)):
-            gain_rows = held.tile([P, P], F32, name=name + "_gain_rows", align_bytes=64)
-            nc.sync.dma_start(gain_rows[:], gain.rearrange("r one -> (r one)").partition_broadcast(P))
-            gain_by_lane = held.tile([P, P], F32, name=name + "_gain_by_lane", align_bytes=64)
-            nc.vector.transpose(gain_by_lane[:], gain_rows[:])
-            gain_of_head.append(gain_by_lane)
-        gain_of_head.insert(0, gain_of_head[0])
 
         zeros = held.tile([P, PIECE], BF16, name="zeros")
         nc.vector.memset(zeros[:], 0.0)
@@ -72,72 +69,67 @@ def tile_cohereattention_kernel(tc, table, w, q_gain, k_gain, offs, out):
             )
             return product
 
-        to_normalise = [(piece, head) for piece in range(PICKED // PIECE) for head in range(VALUE_HEAD)]
+        def store(piece, head, result):
+            nc.sync.dma_start(
+                out[head * P : (head + 1) * P, piece * PIECE : (piece + 1) * PIECE], result[:]
+            )
+
+        to_normalise = [(piece, head) for piece in range(PIECES) for head in range(VALUE_HEAD)]
 
         parked = []
-        for piece, head in to_normalise:
+        for n, (piece, head) in enumerate(to_normalise):
             product = project(piece, head)
-            product_sb = work.tile([P, PIECE], F32, name="product_sb")
-            nc.scalar.activation(
-                product_sb[:].rearrange("r (g q b) -> r g q b", g=FOUR, q=FOUR),
-                product[:].rearrange("r (q g b) -> r g q b", q=FOUR, g=FOUR),
-                ACT.Copy,
-            )
+            product_sb = held.tile([P, PIECE], F32, name=f"product_sb{n}")
+            if n % 2 == 0:
+                nc.scalar.activation(product_sb[:], product[:], ACT.Copy)
+            else:
+                nc.vector.tensor_copy(product_sb[:], product[:])
             parked.append(product_sb)
 
         for (piece, head), product_sb in zip(to_normalise, parked):
-            by_token = psum.tile([P, FOUR, P], F32, name="by_token", tag="bank")
-            for g in range(FOUR):
+            by_token = psum.tile([P, BLOCKS, P], F32, name="by_token", tag="bank")
+            for b in range(BLOCKS):
                 nc.tensor.transpose(
-                    by_token[:, g, :], product_sb[:, g * P : (g + 1) * P], identity[:]
+                    by_token[:, b, :], product_sb[:, b * P : (b + 1) * P], identity[:]
                 )
 
-            stats = small.tile([P, FOUR, 6], F32, name="stats")
-            mean_var = small.tile([P, FOUR, 2], F32, name="mean_var")
-            for g in range(FOUR):
-                nc.vector.bn_stats(stats[:, g, :], by_token[:, g, :])
-                nc.vector.bn_aggr(mean_var[:, g, :], stats[:, g, :])
-            std = small.tile([P, FOUR], F32, name="std")
+            stats = small.tile([P, BLOCKS, 6], F32, name="stats")
+            mean_var = small.tile([P, BLOCKS, 2], F32, name="mean_var")
+            for b in range(BLOCKS):
+                nc.vector.bn_stats(stats[:, b, :], by_token[:, b, :])
+            for b in range(BLOCKS):
+                nc.vector.bn_aggr(mean_var[:, b, :], stats[:, b, :])
+            std = small.tile([P, BLOCKS], F32, name="std")
             nc.scalar.activation(std[:], mean_var[:, :, 1], ACT.Sqrt, bias=eps[:, 0:1])
-            inv_std = small.tile([P, FOUR], F32, name="inv_std")
+            inv_std = small.tile([P, BLOCKS], F32, name="inv_std")
             nc.vector.reciprocal(inv_std[:], std[:])
-            shift = small.tile([P, FOUR], F32, name="shift")
+            shift = small.tile([P, BLOCKS], F32, name="shift")
             nc.vector.scalar_tensor_tensor(
                 shift[:], mean_var[:, :, 0], -1.0, inv_std[:], ALU.mult, ALU.mult
             )
 
-            normed = work.tile([P, FOUR, FOUR, SIDE], F32, name="normed", align_bytes=64)
-            for g in range(FOUR):
+            normed = work.tile([P, BLOCKS, P], F32, name="normed")
+            for b in range(BLOCKS):
                 nc.scalar.activation(
-                    normed[:, :, g, :],
-                    by_token[:, g, :].rearrange("p (c a) -> p c a", c=FOUR),
+                    normed[:, b, :],
+                    by_token[:, b, :],
                     ACT.Identity,
-                    bias=shift[:, g : g + 1],
-                    scale=inv_std[:, g : g + 1],
+                    bias=shift[:, b : b + 1],
+                    scale=inv_std[:, b : b + 1],
                 )
-            flipped = work.tile([P, FOUR, P], F32, name="flipped", align_bytes=64)
-            nc.vector.transpose(
-                flipped[:].rearrange("p c x -> p (c x)"),
-                normed[:].rearrange("p c g a -> p (c g a)"),
+            by_feature = psum.tile([P, PIECE], F32, name="by_feature", bufs=BACK_BANKS)
+            for b in range(BLOCKS):
+                nc.tensor.transpose(
+                    by_feature[:, b * P : (b + 1) * P], normed[:, b, :], identity[:]
+                )
+            result = work.tile([P, PIECE], F32, name="result")
+            nc.scalar.activation(
+                result[:], by_feature[:], ACT.Identity, scale=gain_of_head[head][:, 0:1]
             )
-            result = work.tile([P, FOUR, P], F32, name="result")
-            for c in range(FOUR):
-                nc.vector.tensor_scalar_mul(
-                    result[:, c, :],
-                    flipped[:, c, :],
-                    gain_of_head[head][:, c * SIDE : c * SIDE + 1],
-                )
-            rows = out[head * P : (head + 1) * P, piece * PIECE : (piece + 1) * PIECE]
-            for q in range(FOUR):
-                nc.sync.dma_start(
-                    rows[:, q * P : (q + 1) * P].rearrange("(c a) x -> a c x", c=FOUR),
-                    result[q * SIDE : (q + 1) * SIDE, :, :],
-                )
+            store(piece, head, result)
 
-        for piece in range(PICKED // PIECE):
+        for piece in range(PIECES):
             product = project(piece, VALUE_HEAD)
             value = work.tile([P, PIECE], F32, name="value")
-            nc.scalar.activation(value[:], product[:], ACT.Copy)
-            nc.sync.dma_start(
-                out[VALUE_HEAD * P : HEADS * P, piece * PIECE : (piece + 1) * PIECE], value[:]
-            )
+            nc.vector.tensor_copy(value[:], product[:])
+            store(piece, VALUE_HEAD, value)

@@ -86,27 +86,26 @@ def tile_cohereattention_kernel(tc, table, w, q_gain, k_gain, offs, out):
                 nc.vector.tensor_copy(product_sb[:], product[:])
             parked.append(product_sb)
 
-        for (piece, head), product_sb in zip(to_normalise, parked):
+        for n, ((piece, head), product_sb) in enumerate(zip(to_normalise, parked)):
             by_token = psum.tile([P, BLOCKS, P], F32, name="by_token", tag="bank")
             for b in range(BLOCKS):
                 nc.tensor.transpose(
                     by_token[:, b, :], product_sb[:, b * P : (b + 1) * P], identity[:]
                 )
 
-            stats = small.tile([P, BLOCKS, 6], F32, name="stats")
-            mean_var = small.tile([P, BLOCKS, 2], F32, name="mean_var")
-            for b in range(BLOCKS):
-                nc.vector.bn_stats(stats[:, b, :], by_token[:, b, :])
-            for b in range(BLOCKS):
-                nc.vector.bn_aggr(mean_var[:, b, :], stats[:, b, :])
+            stats = small.tile([P, BLOCKS, 3], F32, name="stats")
+            for b in range(0, BLOCKS, 2):
+                nc.vector.bn_stats(
+                    stats[:, b : b + 2, :], by_token[:, b : b + 2, :].rearrange("p b f -> p f b")
+                )
+            mean = stats[:, :, 1]
+            summed_squares = stats[:, :, 2]
             std = small.tile([P, BLOCKS], F32, name="std")
-            nc.scalar.activation(std[:], mean_var[:, :, 1], ACT.Sqrt, bias=eps[:, 0:1])
+            nc.scalar.activation(std[:], summed_squares, ACT.Sqrt, bias=eps[:, 0:1], scale=1.0 / P)
             inv_std = small.tile([P, BLOCKS], F32, name="inv_std")
             nc.vector.reciprocal(inv_std[:], std[:])
             shift = small.tile([P, BLOCKS], F32, name="shift")
-            nc.vector.scalar_tensor_tensor(
-                shift[:], mean_var[:, :, 0], -1.0, inv_std[:], ALU.mult, ALU.mult
-            )
+            nc.vector.scalar_tensor_tensor(shift[:], mean, -1.0, inv_std[:], ALU.mult, ALU.mult)
 
             normed = work.tile([P, BLOCKS, P], F32, name="normed")
             for b in range(BLOCKS):
@@ -123,13 +122,19 @@ def tile_cohereattention_kernel(tc, table, w, q_gain, k_gain, offs, out):
                     by_feature[:, b * P : (b + 1) * P], normed[:, b, :], identity[:]
                 )
             result = work.tile([P, PIECE], F32, name="result")
-            nc.scalar.activation(
-                result[:], by_feature[:], ACT.Identity, scale=gain_of_head[head][:, 0:1]
-            )
+            if n % 2 == 0:
+                nc.vector.tensor_scalar_mul(result[:], by_feature[:], gain_of_head[head][:, 0:1])
+            else:
+                nc.scalar.activation(
+                    result[:], by_feature[:], ACT.Identity, scale=gain_of_head[head][:, 0:1]
+                )
             store(piece, head, result)
 
         for piece in range(PIECES):
             product = project(piece, VALUE_HEAD)
             value = work.tile([P, PIECE], F32, name="value")
-            nc.vector.tensor_copy(value[:], product[:])
+            if piece % 2 == 0:
+                nc.scalar.activation(value[:], product[:], ACT.Copy)
+            else:
+                nc.vector.tensor_copy(value[:], product[:])
             store(piece, VALUE_HEAD, value)

@@ -19,6 +19,7 @@ PSUM_BANKS = 8
 IN_FLIGHT = 4
 WARM_UP_MATMULS = 10
 BACK_BANKS = 2
+AHEAD = 4
 
 FLOPS = 2 * P * HEADS * P * PICKED
 
@@ -77,7 +78,9 @@ def tile_cohereattention_kernel(tc, table, w, q_gain, k_gain, offs, out):
         to_normalise = [(piece, head) for piece in range(PIECES) for head in range(VALUE_HEAD)]
 
         parked = []
-        for n, (piece, head) in enumerate(to_normalise):
+
+        def project_and_park(n):
+            piece, head = to_normalise[n]
             product = project(piece, head)
             product_sb = held.tile([P, PIECE], F32, name=f"product_sb{n}")
             if n % 2 == 0:
@@ -86,7 +89,9 @@ def tile_cohereattention_kernel(tc, table, w, q_gain, k_gain, offs, out):
                 nc.vector.tensor_copy(product_sb[:], product[:])
             parked.append(product_sb)
 
-        for n, ((piece, head), product_sb) in enumerate(zip(to_normalise, parked)):
+        def layer_norm(n):
+            piece, head = to_normalise[n]
+            product_sb = parked[n]
             by_token = psum.tile([P, BLOCKS, P], F32, name="by_token", tag="bank")
             for b in range(BLOCKS):
                 nc.tensor.transpose(
@@ -129,6 +134,13 @@ def tile_cohereattention_kernel(tc, table, w, q_gain, k_gain, offs, out):
                     result[:], by_feature[:], ACT.Identity, scale=gain_of_head[head][:, 0:1]
                 )
             store(piece, head, result)
+
+        for n in range(AHEAD):
+            project_and_park(n)
+        for n in range(len(to_normalise)):
+            layer_norm(n)
+            if n + AHEAD < len(to_normalise):
+                project_and_park(n + AHEAD)
 
         for piece in range(PIECES):
             product = project(piece, VALUE_HEAD)

@@ -19,7 +19,7 @@ PSUM_BANKS = 8
 IN_FLIGHT = 4
 WARM_UP_MATMULS = 10
 BACK_BANKS = 2
-AHEAD = 4
+AHEAD = 3
 
 FLOPS = 2 * P * HEADS * P * PICKED
 
@@ -75,22 +75,24 @@ def tile_cohereattention_kernel(tc, table, w, q_gain, k_gain, offs, out):
                 out[head * P : (head + 1) * P, piece * PIECE : (piece + 1) * PIECE], result[:]
             )
 
-        to_normalise = [(piece, head) for piece in range(PIECES) for head in range(VALUE_HEAD)]
+        products = [(piece, head) for piece in range(PIECES) for head in range(HEADS)]
+        parked = {}
+        measured = {}
 
-        parked = []
-
-        def project_and_park(n):
-            piece, head = to_normalise[n]
+        def project_and_copy(n):
+            piece, head = products[n]
             product = project(piece, head)
             product_sb = held.tile([P, PIECE], F32, name=f"product_sb{n}")
             if n % 2 == 0:
                 nc.scalar.activation(product_sb[:], product[:], ACT.Copy)
             else:
                 nc.vector.tensor_copy(product_sb[:], product[:])
-            parked.append(product_sb)
+            if head == VALUE_HEAD:
+                store(piece, head, product_sb)
+            else:
+                parked[n] = product_sb
 
-        def layer_norm(n):
-            piece, head = to_normalise[n]
+        def flip_and_measure(n):
             product_sb = parked[n]
             by_token = psum.tile([P, BLOCKS, P], F32, name="by_token", tag="bank")
             for b in range(BLOCKS):
@@ -111,7 +113,11 @@ def tile_cohereattention_kernel(tc, table, w, q_gain, k_gain, offs, out):
             nc.vector.reciprocal(inv_std[:], std[:])
             shift = small.tile([P, BLOCKS], F32, name="shift")
             nc.vector.scalar_tensor_tensor(shift[:], mean, -1.0, inv_std[:], ALU.mult, ALU.mult)
+            measured[n] = (by_token, inv_std, shift)
 
+        def normalise_and_store(n):
+            piece, head = products[n]
+            by_token, inv_std, shift = measured[n]
             normed = work.tile([P, BLOCKS, P], F32, name="normed")
             for b in range(BLOCKS):
                 nc.scalar.activation(
@@ -135,18 +141,10 @@ def tile_cohereattention_kernel(tc, table, w, q_gain, k_gain, offs, out):
                 )
             store(piece, head, result)
 
-        for n in range(AHEAD):
-            project_and_park(n)
-        for n in range(len(to_normalise)):
-            layer_norm(n)
-            if n + AHEAD < len(to_normalise):
-                project_and_park(n + AHEAD)
-
-        for piece in range(PIECES):
-            product = project(piece, VALUE_HEAD)
-            value = work.tile([P, PIECE], F32, name="value")
-            if piece % 2 == 0:
-                nc.scalar.activation(value[:], product[:], ACT.Copy)
-            else:
-                nc.vector.tensor_copy(value[:], product[:])
-            store(piece, VALUE_HEAD, value)
+        for step in range(len(products) + AHEAD + 1):
+            if step - AHEAD in parked:
+                flip_and_measure(step - AHEAD)
+            if step - AHEAD - 1 in measured:
+                normalise_and_store(step - AHEAD - 1)
+            if step < len(products):
+                project_and_copy(step)

@@ -111,6 +111,10 @@ def tile_cohereattention_kernel(tc, table, w, q_gain, k_gain, offs, out):
             nc.scalar.activation(std[:], summed_squares, ACT.Sqrt, bias=eps[:, 0:1], scale=1.0 / P)
             inv_std = small.tile([P, BLOCKS], F32, name="inv_std")
             nc.vector.reciprocal(inv_std[:], std[:])
+            measured[n] = (by_token, mean, inv_std)
+
+        def make_shift(n):
+            by_token, mean, inv_std = measured[n]
             shift = small.tile([P, BLOCKS], F32, name="shift")
             nc.vector.scalar_tensor_tensor(shift[:], mean, -1.0, inv_std[:], ALU.mult, ALU.mult)
             measured[n] = (by_token, inv_std, shift)
@@ -142,6 +146,8 @@ def tile_cohereattention_kernel(tc, table, w, q_gain, k_gain, offs, out):
             store(piece, head, result)
 
         for step in range(len(products) + AHEAD + 1):
+            if step - AHEAD - 1 in measured:
+                make_shift(step - AHEAD - 1)
             if step - AHEAD in parked:
                 flip_and_measure(step - AHEAD)
             if step - AHEAD - 1 in measured:

@@ -99,37 +99,33 @@ def tile_cohereattention_kernel(tc, table, w, q_gain, k_gain, offs, out):
                 nc.tensor.transpose(
                     by_token[:, b, :], product_sb[:, b * P : (b + 1) * P], identity[:]
                 )
+            by_token_sb = work.tile([P, BLOCKS, P], F32, name="by_token_sb")
+            nc.scalar.activation(by_token_sb[:], by_token[:], ACT.Copy)
 
             stats = small.tile([P, BLOCKS, 3], F32, name="stats")
             for b in range(0, BLOCKS, 2):
                 nc.vector.bn_stats(
-                    stats[:, b : b + 2, :], by_token[:, b : b + 2, :].rearrange("p b f -> p f b")
+                    stats[:, b : b + 2, :], by_token_sb[:, b : b + 2, :].rearrange("p b f -> p f b")
                 )
-            mean = stats[:, :, 1]
             summed_squares = stats[:, :, 2]
             std = small.tile([P, BLOCKS], F32, name="std")
             nc.scalar.activation(std[:], summed_squares, ACT.Sqrt, bias=eps[:, 0:1], scale=1.0 / P)
             inv_std = small.tile([P, BLOCKS], F32, name="inv_std")
             nc.vector.reciprocal(inv_std[:], std[:])
-            measured[n] = (by_token, mean, inv_std)
-
-        def make_shift(n):
-            by_token, mean, inv_std = measured[n]
-            shift = small.tile([P, BLOCKS], F32, name="shift")
-            nc.vector.scalar_tensor_tensor(shift[:], mean, -1.0, inv_std[:], ALU.mult, ALU.mult)
-            measured[n] = (by_token, inv_std, shift)
+            measured[n] = (by_token_sb, stats, inv_std)
 
         def normalise_and_store(n):
             piece, head = products[n]
-            by_token, inv_std, shift = measured[n]
+            by_token_sb, stats, inv_std = measured[n]
             normed = work.tile([P, BLOCKS, P], F32, name="normed")
             for b in range(BLOCKS):
-                nc.scalar.activation(
+                nc.vector.tensor_scalar(
                     normed[:, b, :],
-                    by_token[:, b, :],
-                    ACT.Identity,
-                    bias=shift[:, b : b + 1],
-                    scale=inv_std[:, b : b + 1],
+                    by_token_sb[:, b, :],
+                    stats[:, b, 1:2],
+                    inv_std[:, b : b + 1],
+                    ALU.subtract,
+                    ALU.mult,
                 )
             by_feature = psum.tile([P, PIECE], F32, name="by_feature", bufs=BACK_BANKS)
             for b in range(BLOCKS):
@@ -137,20 +133,15 @@ def tile_cohereattention_kernel(tc, table, w, q_gain, k_gain, offs, out):
                     by_feature[:, b * P : (b + 1) * P], normed[:, b, :], identity[:]
                 )
             result = work.tile([P, PIECE], F32, name="result")
-            if n % 2 == 0:
-                nc.vector.tensor_scalar_mul(result[:], by_feature[:], gain_of_head[head][:, 0:1])
-            else:
-                nc.scalar.activation(
-                    result[:], by_feature[:], ACT.Identity, scale=gain_of_head[head][:, 0:1]
-                )
+            nc.scalar.activation(
+                result[:], by_feature[:], ACT.Identity, scale=gain_of_head[head][:, 0:1]
+            )
             store(piece, head, result)
 
         for step in range(len(products) + AHEAD + 1):
             if step - AHEAD - 1 in measured:
-                make_shift(step - AHEAD - 1)
+                normalise_and_store(step - AHEAD - 1)
             if step - AHEAD in parked:
                 flip_and_measure(step - AHEAD)
-            if step - AHEAD - 1 in measured:
-                normalise_and_store(step - AHEAD - 1)
             if step < len(products):
                 project_and_copy(step)

@@ -16,7 +16,7 @@ HEADS = 4
 VALUE_HEAD = 3
 EPS = 1e-5
 PSUM_BANKS = 8
-IN_FLIGHT = 4
+IN_FLIGHT = 8
 WARM_UP_MATMULS = 10
 BACK_BANKS = 2
 AHEAD = 3

@@ -18,7 +18,8 @@ EPS = 1e-5
 PSUM_BANKS = 8
 IN_FLIGHT = 8
 WARM_UP_MATMULS = 10
-BACK_BANKS = 2
+HOLDING_MATMULS = 2
+BACK_BANKS = 3
 AHEAD = 3
 
 FLOPS = 2 * P * HEADS * P * PICKED
@@ -58,6 +59,11 @@ def tile_cohereattention_kernel(tc, table, w, q_gain, k_gain, offs, out):
         unread = psum.tile([P, PIECE], F32, name="unread", tag="bank")
         for step in range(WARM_UP_MATMULS):
             nc.tensor.matmul(unread[:], zeros[:, :P], zeros[:], start=True, stop=True)
+
+        def hold_the_clock():
+            unread_late = psum.tile([P, PIECE], F32, name="unread_late", tag="by_feature", bufs=BACK_BANKS)
+            for repeat in range(HOLDING_MATMULS):
+                nc.tensor.matmul(unread_late[:], zeros[:, :P], zeros[:], start=True, stop=True)
 
         def project(piece, head):
             product = psum.tile([P, PIECE], F32, name="product", tag="bank")
@@ -140,6 +146,8 @@ def tile_cohereattention_kernel(tc, table, w, q_gain, k_gain, offs, out):
 
         for step in range(len(products) + AHEAD + 1):
             if step - AHEAD - 1 in measured:
+                if step >= len(products):
+                    hold_the_clock()
                 normalise_and_store(step - AHEAD - 1)
             if step - AHEAD in parked:
                 flip_and_measure(step - AHEAD)

@@ -17,7 +17,7 @@ VALUE_HEAD = 3
 EPS = 1e-5
 PSUM_BANKS = 8
 IN_FLIGHT = 8
-WARM_UP_MATMULS = 10
+WARM_UP_MATMULS = 6
 HOLDING_MATMULS = 2
 BACK_BANKS = 3
 AHEAD = 3
@@ -33,14 +33,14 @@ def tile_cohereattention_kernel(tc, table, w, q_gain, k_gain, offs, out):
         tc.tile_pool(name="small", bufs=IN_FLIGHT) as small,
         tc.psum_pool(name="psum", bufs=PSUM_BANKS - BACK_BANKS) as psum,
     ):
-        offsets = held.tile([P, PICKED // 16], U16, name="offsets")
-        nc.sync.dma_start(offsets[:], offs)
-        weights = held.tile([P, HEADS * P], BF16, name="weights")
-        nc.scalar.dma_start(weights[:], w)
         window = held.tile([P, TABLE_COLUMNS], BF16, name="window")
         half = TABLE_COLUMNS // 2
         nc.sync.dma_start(window[:, :half], table[:, :half])
-        nc.scalar.dma_start(window[:, half:], table[:, half:])
+        nc.sync.dma_start(window[:, half:], table[:, half:])
+        offsets = held.tile([P, PICKED // 16], U16, name="offsets")
+        nc.sync.dma_start(offsets[:], offs)
+        weights = held.tile([P, HEADS * P], BF16, name="weights")
+        nc.sync.dma_start(weights[:], w)
         query_gain = held.tile([P, 1], F32, name="query_gain")
         nc.sync.dma_start(query_gain[:], q_gain)
         key_gain = held.tile([P, 1], F32, name="key_gain")

import concourse.mybir as mybir
from concourse.masks import make_identity

BF16, F32, U16 = mybir.dt.bfloat16, mybir.dt.float32, mybir.dt.uint16
ALU = mybir.AluOpType
ACT = mybir.ActivationFunctionType

P = 128
TABLE_COLUMNS = 4096
PICKED = 2048
PIECE = 512
PIECES = PICKED // PIECE
BLOCKS = PIECE // P
OFFSET_COLUMNS = PIECE // 16
HEADS = 4
VALUE_HEAD = 3
EPS = 1e-5
PSUM_BANKS = 8
IN_FLIGHT = 8
WARM_UP_MATMULS = 6
HOLDING_MATMULS = 2
BACK_BANKS = 3
AHEAD = 3

FLOPS = 2 * P * HEADS * P * PICKED


def tile_cohereattention_kernel(tc, table, w, q_gain, k_gain, offs, out):
    nc = tc.nc
    with (
        tc.tile_pool(name="held", bufs=1) as held,
        tc.tile_pool(name="work", bufs=IN_FLIGHT) as work,
        tc.tile_pool(name="small", bufs=IN_FLIGHT) as small,
        tc.psum_pool(name="psum", bufs=PSUM_BANKS - BACK_BANKS) as psum,
    ):
        window = held.tile([P, TABLE_COLUMNS], BF16, name="window")
        half = TABLE_COLUMNS // 2
        nc.sync.dma_start(window[:, :half], table[:, :half])
        nc.sync.dma_start(window[:, half:], table[:, half:])
        offsets = held.tile([P, PICKED // 16], U16, name="offsets")
        nc.sync.dma_start(offsets[:], offs)
        weights = held.tile([P, HEADS * P], BF16, name="weights")
        nc.sync.dma_start(weights[:], w)
        query_gain = held.tile([P, 1], F32, name="query_gain")
        nc.sync.dma_start(query_gain[:], q_gain)
        key_gain = held.tile([P, 1], F32, name="key_gain")
        nc.sync.dma_start(key_gain[:], k_gain)
        gain_of_head = [query_gain, query_gain, key_gain]

        identity = held.tile([P, P], F32, name="identity")
        make_identity(nc, identity[:])
        eps = held.tile([P, 1], F32, name="eps")
        nc.vector.memset(eps[:], EPS)
        scratch = held.tile([P, 1], F32, name="scratch")
        nc.scalar.activation(scratch[:], eps[:], ACT.Sqrt)

        zeros = held.tile([P, PIECE], BF16, name="zeros")
        nc.vector.memset(zeros[:], 0.0)
        unread = psum.tile([P, PIECE], F32, name="unread", tag="bank")
        for step in range(WARM_UP_MATMULS):
            nc.tensor.matmul(unread[:], zeros[:, :P], zeros[:], start=True, stop=True)

        def hold_the_clock():
            unread_late = psum.tile([P, PIECE], F32, name="unread_late", tag="by_feature", bufs=BACK_BANKS)
            for repeat in range(HOLDING_MATMULS):
                nc.tensor.matmul(unread_late[:], zeros[:, :P], zeros[:], start=True, stop=True)

        def project(piece, head):
            product = psum.tile([P, PIECE], F32, name="product", tag="bank")
            nc.tensor.matmul(
                product[:],
                weights[:, head * P : (head + 1) * P],
                window[:].indirect(offsets[:, piece * OFFSET_COLUMNS : (piece + 1) * OFFSET_COLUMNS]),
                start=True,
                stop=True,
            )
            return product

        def store(piece, head, result):
            nc.sync.dma_start(
                out[head * P : (head + 1) * P, piece * PIECE : (piece + 1) * PIECE], result[:]
            )

        products = [(piece, head) for piece in range(PIECES) for head in range(HEADS)]
        parked = {}
        measured = {}

        def project_and_copy(n):
            piece, head = products[n]
            product = project(piece, head)
            product_sb = held.tile([P, PIECE], F32, name=f"product_sb{n}")
            if n % 2 == 0:
                nc.scalar.activation(product_sb[:], product[:], ACT.Copy)
            else:
                nc.vector.tensor_copy(product_sb[:], product[:])
            if head == VALUE_HEAD:
                store(piece, head, product_sb)
            else:
                parked[n] = product_sb

        def flip_and_measure(n):
            product_sb = parked[n]
            by_token = psum.tile([P, BLOCKS, P], F32, name="by_token", tag="bank")
            for b in range(BLOCKS):
                nc.tensor.transpose(
                    by_token[:, b, :], product_sb[:, b * P : (b + 1) * P], identity[:]
                )
            by_token_sb = work.tile([P, BLOCKS, P], F32, name="by_token_sb")
            nc.scalar.activation(by_token_sb[:], by_token[:], ACT.Copy)

            stats = small.tile([P, BLOCKS, 3], F32, name="stats")
            for b in range(0, BLOCKS, 2):
                nc.vector.bn_stats(
                    stats[:, b : b + 2, :], by_token_sb[:, b : b + 2, :].rearrange("p b f -> p f b")
                )
            summed_squares = stats[:, :, 2]
            std = small.tile([P, BLOCKS], F32, name="std")
            nc.scalar.activation(std[:], summed_squares, ACT.Sqrt, bias=eps[:, 0:1], scale=1.0 / P)
            inv_std = small.tile([P, BLOCKS], F32, name="inv_std")
            nc.vector.reciprocal(inv_std[:], std[:])
            measured[n] = (by_token_sb, stats, inv_std)

        def normalise_and_store(n):
            piece, head = products[n]
            by_token_sb, stats, inv_std = measured[n]
            normed = work.tile([P, BLOCKS, P], F32, name="normed")
            for b in range(BLOCKS):
                nc.vector.tensor_scalar(
                    normed[:, b, :],
                    by_token_sb[:, b, :],
                    stats[:, b, 1:2],
                    inv_std[:, b : b + 1],
                    ALU.subtract,
                    ALU.mult,
                )
            by_feature = psum.tile([P, PIECE], F32, name="by_feature", bufs=BACK_BANKS)
            for b in range(BLOCKS):
                nc.tensor.transpose(
                    by_feature[:, b * P : (b + 1) * P], normed[:, b, :], identity[:]
                )
            result = work.tile([P, PIECE], F32, name="result")
            nc.scalar.activation(
                result[:], by_feature[:], ACT.Identity, scale=gain_of_head[head][:, 0:1]
            )
            store(piece, head, result)

        for step in range(len(products) + AHEAD + 1):
            if step - AHEAD - 1 in measured:
                if step >= len(products):
                    hold_the_clock()
                normalise_and_store(step - AHEAD - 1)
            if step - AHEAD in parked:
                flip_and_measure(step - AHEAD)
            if step < len(products):
                project_and_copy(step)
